import numpy as np
import ml_dtypes


def mxq(x, axis, fmt="e4m3"):
    dtype, down = {"e4m3": (ml_dtypes.float8_e4m3fn, 7), "e5m2": (ml_dtypes.float8_e5m2, 14)}[fmt]
    v = np.moveaxis(np.asarray(x, np.float32).astype(ml_dtypes.bfloat16).astype(np.float64), axis, -1)
    blocks = v.reshape(v.shape[:-1] + (-1, 32))
    amax = np.abs(blocks).max(-1, keepdims=True)
    byte = np.maximum(np.where(amax > 0, np.frexp(amax)[1] - 1 + 127, 0) - down, 1)
    scale = np.exp2(byte - 127.0)
    codes = (blocks / scale).astype(np.float32).astype(dtype).astype(np.float64)
    return np.moveaxis((codes * scale).reshape(v.shape), -1, axis)


WIDE = False


def mx_kscale(k):
    if not WIDE:
        return np.ones(k)
    levels = np.array([10, -10, 5, -5, 0])
    a = np.random.permutation(np.resize(levels, k // 512 * 4)).reshape(k // 512, 4)
    idx = np.arange(k)
    return np.exp2(a[idx // 512, idx % 128 // 32])


BF16 = ml_dtypes.bfloat16


def bf(x):
    return np.asarray(x, np.float32).astype(BF16)


def f64(x):
    return np.asarray(x).astype(np.float64)


B, L, H, G, DEPTH = 64, 64, 1024, 256, 3
EPS = 1e-5


def layernorm(v, g, b):
    mu = v.mean(-1, keepdims=True)
    var = np.square(v - mu).mean(-1, keepdims=True)
    return (v - mu) / np.sqrt(var + EPS) * g + b


def setup_inputs():
    s, t = mx_kscale(H), mx_kscale(H)
    return {"x_nodes": bf(np.random.standard_normal((B, L, H)) * s),
            "w1": bf(np.random.standard_normal((H, H)) / np.sqrt(H) / s[:, None]),
            "b1": bf(np.random.standard_normal(H) * 0.3),
            "gamma": bf((1.0 + 0.1 * np.random.standard_normal(H)) * t),
            "beta": bf(0.2 * np.random.standard_normal(H) * t),
            "w2": bf(np.random.standard_normal((H, G)) / np.sqrt(H) / t[:, None]),
            "b2": bf(np.random.standard_normal(G) * 0.3)}


def reference(x_nodes, w1, b1, gamma, beta, w2, b2):
    h = (mxq(f64(x_nodes), 2, "e4m3") @ mxq(f64(w1), 0, "e4m3")) + f64(b1)
    r = np.maximum(layernorm(h, f64(gamma), f64(beta)), 0.0)
    x1 = (mxq(r, 2, "e4m3") @ mxq(f64(w2), 0, "e4m3")) + f64(b2)
    x2 = np.broadcast_to(x1.max(axis=1, keepdims=True), x1.shape)
    x = np.concatenate([x1, x2], axis=2)
    return x.max(axis=1)

@@ -1,0 +1,311 @@
+from contextlib import ExitStack
+
+import concourse.mybir as mybir
+from concourse.masks import make_identity
+
+F32 = mybir.dt.float32
+BF16 = mybir.dt.bfloat16
+U32 = mybir.dt.uint32
+U8 = mybir.dt.uint8
+FP8X4 = mybir.dt.float8_e4m3fn_x4
+ACT = mybir.ActivationFunctionType
+ALU = mybir.AluOpType
+AX = mybir.AxisListType
+
+P = 128
+PACK = 4
+K_PASS = P * PACK
+BANK = 512
+
+TOKENS = 64 * 64
+NODES = 64
+H = 1024
+G = 256
+EPS = 1e-5
+PASSES = H // K_PASS
+TILES = 4
+BLOCK = TILES * P
+N_BLOCKS = TOKENS // BLOCK
+CHUNKS = H // P
+HALVES = H // BANK
+
+FLOPS = 2 * TOKENS * H * H + 2 * TOKENS * H * G
+
+
+def regroup(nc, grouped, planes):
+    nc.vector.tensor_copy(
+        out=grouped.rearrange("p (c i) t -> p c t i", i=4),
+        in_=planes.rearrange("p t (c i) -> p c t i", i=4),
+    )
+
+
+def tile_sub_graph_pb_t_kernel(tc, x_nodes, w1, b1, gamma, beta, w2, b2, out):
+    nc = tc.nc
+    x = x_nodes.rearrange("b l k -> (b l) k")
+
+    with ExitStack() as ctx:
+        const = ctx.enter_context(tc.tile_pool(name="const", bufs=1))
+        wstage = ctx.enter_context(tc.tile_pool(name="wstage", bufs=2))
+        xpool = ctx.enter_context(tc.tile_pool(name="xpool", bufs=2))
+        hpool = ctx.enter_context(tc.tile_pool(name="hpool", bufs=3))
+        stat = ctx.enter_context(tc.tile_pool(name="stat", bufs=3))
+        rpool = ctx.enter_context(tc.tile_pool(name="rpool", bufs=2))
+        psum = ctx.enter_context(tc.psum_pool(name="psum", bufs=1))
+
+        w1_raws = {}
+        for g in range(PASSES):
+            w1_raw = wstage.tile([P, PACK, H], BF16, tag="w1_raw")
+            for u in range(2):
+                k0 = K_PASS * g + 256 * u
+                nc.sync.dma_start(
+                    out=w1_raw[:, 2 * u : 2 * u + 2, :],
+                    in_=w1[k0 : k0 + 256, :].rearrange("(p e) c -> p e c", e=2),
+                )
+            w1_raws[g] = w1_raw
+
+        x_tiles = {}
+
+        def load_x(blk):
+            x_sb = xpool.tile([P, TILES * H], BF16, tag="x_sb", bufs=3)
+            nc.sync.dma_start(
+                out=x_sb[:].rearrange("p (i k) -> p i k", i=TILES),
+                in_=x[blk * BLOCK : (blk + 1) * BLOCK, :].rearrange("(i p) k -> p i k", p=P),
+            )
+            x_tiles[blk] = x_sb
+
+        load_x(0)
+        load_x(1)
+        w2_raw = const.tile([P, CHUNKS, G], BF16)
+        nc.sync.dma_start(out=w2_raw[:], in_=w2.rearrange("(a p) n -> p a n", p=P))
+
+        ident = const.tile([P, P], F32)
+        make_identity(nc, ident[:])
+        eps_col = const.tile([P, 1], F32)
+        nc.vector.memset(eps_col[:], EPS)
+        warm = const.tile([P, 1], F32)
+        nc.scalar.activation(out=warm[:], in_=eps_col[:], func=ACT.Sqrt)
+
+        rows = const.tile([P, P], BF16)
+        nc.vector.memset(rows[:], 0.0)
+        nc.scalar.dma_start(out=rows[0:CHUNKS, :], in_=gamma.rearrange("(c p) -> c p", p=P))
+        nc.scalar.dma_start(
+            out=rows[CHUNKS : 2 * CHUNKS, :], in_=beta.rearrange("(c p) -> c p", p=P)
+        )
+        nc.scalar.dma_start(
+            out=rows[2 * CHUNKS : 2 * CHUNKS + 2, :], in_=b2.rearrange("(c p) -> c p", p=P)
+        )
+        rows_f32 = const.tile([P, P], F32)
+        nc.vector.tensor_copy(out=rows_f32[:], in_=rows[:])
+        cols_ps = psum.tile([P, P], F32, tag="xT", bufs=2)
+        nc.tensor.transpose(cols_ps[:], rows_f32[:], ident[:])
+        cols = const.tile([P, 2 * CHUNKS + 2], F32)
+        nc.vector.tensor_copy(out=cols[:], in_=cols_ps[:, 0 : 2 * CHUNKS + 2])
+        gamma_col = cols[:, 0:CHUNKS]
+        beta_col = cols[:, CHUNKS : 2 * CHUNKS]
+        b2_col = cols[:, 2 * CHUNKS : 2 * CHUNKS + 2]
+
+        b1_row = const.tile([P, H], BF16)
+        nc.vector.memset(b1_row[:], 0.0)
+        nc.scalar.dma_start(out=b1_row[0:1, :], in_=b1.rearrange("(o h) -> o h", o=1))
+        ones = const.tile([P, P], BF16)
+        nc.vector.memset(ones[:], 1.0)
+        b1_all = const.tile([P, H], F32)
+        for n in range(HALVES):
+            b1_ps = psum.tile([P, BANK], F32, tag="h_ps", bufs=3)
+            nc.tensor.matmul(
+                out=b1_ps[:], lhsT=ones[:], rhs=b1_row[:, n * BANK : (n + 1) * BANK],
+                start=True, stop=True,
+            )
+            nc.scalar.copy(out=b1_all[:, n * BANK : (n + 1) * BANK], in_=b1_ps[:])
+
+        w1_codes = const.tile([P, PASSES, H], U32, align_bytes=64)
+        w1_scales = const.tile([P, PASSES, H], U8, align_bytes=64)
+        for g in range(PASSES):
+            for n in range(HALVES):
+                cols_n = slice(n * BANK, (n + 1) * BANK)
+                w1_grp = wstage.tile([P, BANK, PACK], BF16, tag="w1_grp", align_bytes=64)
+                regroup(nc, w1_grp[:], w1_raws[g][:, :, cols_n])
+                nc.vector.quantize_mx(
+                    out=w1_codes[:, g, cols_n].bitcast(FP8X4),
+                    scales=w1_scales[:, g, cols_n],
+                    in_=w1_grp[:].rearrange("p c t -> p (c t)"),
+                )
+
+        w2_grp = const.tile([P, PASSES, G, PACK], BF16, align_bytes=64)
+        w2_codes = const.tile([P, PASSES, G], U32, align_bytes=64)
+        w2_scales = const.tile([P, PASSES, G], U8, align_bytes=64)
+        for g in range(PASSES):
+            regroup(nc, w2_grp[:, g, :, :], w2_raw[:, PACK * g : PACK * (g + 1), :])
+        nc.vector.quantize_mx(
+            out=w2_codes[:].rearrange("p g c -> p (g c)").bitcast(FP8X4),
+            scales=w2_scales[:].rearrange("p g c -> p (g c)"),
+            in_=w2_grp[:].rearrange("p g c t -> p (g c t)"),
+        )
+
+        node_max = const.tile([P, 2, TOKENS // NODES], F32)
+
+        x_quant = {}
+
+        def transpose_and_quantise_x(blk):
+            x_words = x_tiles[blk][:].bitcast(F32)
+            x_grp = xpool.tile([P, TILES * H], BF16, tag="x_grp", align_bytes=64)
+            x_grp_words = x_grp[:].bitcast(F32)
+            for i in range(TILES):
+                xT_ps = psum.tile([P, PACK, P], F32, tag="xT", bufs=2)
+                for q in range(PACK):
+                    w0 = i * (H // 2) + q * P
+                    nc.tensor.transpose(xT_ps[:, q, :], x_words[:, w0 : w0 + P], ident[:])
+                nc.scalar.copy(
+                    out=x_grp_words[:, i * (H // 2) : (i + 1) * (H // 2)].rearrange(
+                        "p (g w u) -> p g w u", g=PASSES, u=2
+                    ),
+                    in_=xT_ps[:].rearrange("p (g u) w -> p g w u", g=PASSES),
+                )
+            x_codes = xpool.tile([P, TILES, PASSES, P], U32, tag="x_codes", align_bytes=64)
+            x_scales = xpool.tile([P, TILES, PASSES, P], U8, tag="x_scales", align_bytes=64)
+            nc.vector.quantize_mx(
+                out=x_codes[:].rearrange("p i g w -> p (i g w)").bitcast(FP8X4),
+                scales=x_scales[:].rearrange("p i g w -> p (i g w)"),
+                in_=x_grp[:],
+            )
+            x_quant[blk] = (x_codes, x_scales)
+
+        def hidden_layer(blk):
+            x_codes, x_scales = x_quant[blk]
+            h_sb = hpool.tile([P, TILES, H], F32, tag="h_sb")
+            h_sum = stat.tile([P, TILES, HALVES], F32, tag="h_sum")
+            neg_mean = stat.tile([P, TILES], F32, tag="neg_mean")
+            sq_sum = stat.tile([P, TILES], F32, tag="sq_sum")
+            for i in range(TILES):
+                for n in range(HALVES):
+                    cols_n = slice(n * BANK, (n + 1) * BANK)
+                    h_ps = psum.tile([P, BANK], F32, tag="h_ps", bufs=3)
+                    for g in range(PASSES):
+                        nc.tensor.matmul_mx(
+                            out=h_ps[:],
+                            lhsT=x_codes[:, i, g, :].bitcast(FP8X4),
+                            lhsT_scale=x_scales[:, i, g, :],
+                            rhs=w1_codes[:, g, cols_n].bitcast(FP8X4),
+                            rhs_scale=w1_scales[:, g, cols_n],
+                            start=(g == 0),
+                            stop=(g == PASSES - 1),
+                        )
+                    nc.vector.scalar_tensor_tensor(
+                        out=h_sb[:, i, cols_n],
+                        in0=h_ps[:],
+                        scalar=1.0,
+                        in1=b1_all[:, cols_n],
+                        op0=ALU.mult,
+                        op1=ALU.add,
+                        accum_out=h_sum[:, i, n : n + 1],
+                    )
+                nc.vector.tensor_scalar(
+                    out=neg_mean[:, i : i + 1],
+                    in0=h_sum[:, i, 0:1],
+                    scalar1=h_sum[:, i, 1:2],
+                    scalar2=-1.0 / H,
+                    op0=ALU.add,
+                    op1=ALU.mult,
+                )
+                squares = hpool.tile([P, H], BF16, tag="squares", bufs=2)
+                nc.scalar.activation(
+                    out=squares[:],
+                    in_=h_sb[:, i, :],
+                    func=ACT.Square,
+                    bias=neg_mean[:, i : i + 1],
+                    scale=1.0,
+                    accum_out=sq_sum[:, i : i + 1],
+                )
+            return h_sb, neg_mean, sq_sum
+
+        def normalise(h_sb, neg_mean, sq_sum):
+            std = stat.tile([P, TILES], F32, tag="std")
+            nc.scalar.activation(
+                out=std[:], in_=sq_sum[:], func=ACT.Sqrt, bias=eps_col[:, 0:1], scale=1.0 / H
+            )
+            rstd = stat.tile([P, TILES], F32, tag="rstd")
+            nc.vector.reciprocal(out=rstd[:], in_=std[:])
+            for i in range(TILES):
+                nc.gpsimd.tensor_scalar(
+                    out=h_sb[:, i, :],
+                    in0=h_sb[:, i, :],
+                    scalar1=neg_mean[:, i : i + 1],
+                    scalar2=rstd[:, i : i + 1],
+                    op0=ALU.add,
+                    op1=ALU.mult,
+                )
+
+        def activate_and_quantise(h_sb):
+            r_planes = rpool.tile([P, CHUNKS, BLOCK], BF16, tag="r_planes")
+            r_grp = rpool.tile([P, PASSES, BLOCK, PACK], BF16, tag="r_grp", align_bytes=64)
+            r_codes = rpool.tile([P, PASSES, BLOCK], U32, tag="r_codes", align_bytes=64)
+            r_scales = rpool.tile([P, PASSES, BLOCK], U8, tag="r_scales", align_bytes=64)
+            for g in range(PASSES):
+                for j in range(PACK):
+                    c = PACK * g + j
+                    nT_ps = psum.tile([P, BLOCK], F32, tag="nT", bufs=2)
+                    for i in range(TILES):
+                        nc.tensor.transpose(
+                            nT_ps[:, i * P : (i + 1) * P], h_sb[:, i, c * P : (c + 1) * P], ident[:]
+                        )
+                    nc.scalar.activation(
+                        out=r_planes[:, c, :],
+                        in_=nT_ps[:],
+                        func=ACT.Relu,
+                        bias=beta_col[:, c : c + 1],
+                        scale=gamma_col[:, c : c + 1],
+                    )
+                regroup(nc, r_grp[:, g, :, :], r_planes[:, PACK * g : PACK * (g + 1), :])
+            for g in range(PASSES):
+                nc.vector.quantize_mx(
+                    out=r_codes[:, g, :].bitcast(FP8X4),
+                    scales=r_scales[:, g, :],
+                    in_=r_grp[:, g, :, :].rearrange("p w j -> p (w j)"),
+                )
+            return r_codes, r_scales
+
+        def read_out(blk, r_codes, r_scales):
+            lines = BLOCK // NODES
+            for cc in range(G // P):
+                x1_ps = psum.tile([P, BLOCK], F32, tag="x1", bufs=1)
+                for g in range(PASSES):
+                    nc.tensor.matmul_mx(
+                        out=x1_ps[:],
+                        lhsT=w2_codes[:, g, cc * P : (cc + 1) * P].bitcast(FP8X4),
+                        lhsT_scale=w2_scales[:, g, cc * P : (cc + 1) * P],
+                        rhs=r_codes[:, g, :].bitcast(FP8X4),
+                        rhs_scale=r_scales[:, g, :],
+                        start=(g == 0),
+                        stop=(g == PASSES - 1),
+                    )
+                nc.vector.tensor_reduce(
+                    out=node_max[:, cc, blk * lines : (blk + 1) * lines],
+                    in_=x1_ps[:].rearrange("p (q l) -> p q l", l=NODES),
+                    axis=AX.X,
+                    op=ALU.max,
+                )
+
+        transpose_and_quantise_x(0)
+        for blk in range(N_BLOCKS):
+            if blk + 2 < N_BLOCKS:
+                load_x(blk + 2)
+            if blk + 1 < N_BLOCKS:
+                transpose_and_quantise_x(blk + 1)
+            h_sb, neg_mean, sq_sum = hidden_layer(blk)
+            normalise(h_sb, neg_mean, sq_sum)
+            r_codes, r_scales = activate_and_quantise(h_sb)
+            read_out(blk, r_codes, r_scales)
+
+        for cc in range(G // P):
+            nc.vector.tensor_scalar_add(
+                out=node_max[:, cc, :], in0=node_max[:, cc, :], scalar1=b2_col[:, cc : cc + 1]
+            )
+        maxT_ps = psum.tile([P, P], F32, tag="xT", bufs=2)
+        nc.tensor.transpose(maxT_ps[:], node_max[:].rearrange("p c b -> p (c b)"), ident[:])
+        result = const.tile([P, 2, P], F32)
+        for rep in range(2):
+            nc.vector.tensor_copy(out=result[:, rep, :], in_=maxT_ps[:])
+        out_view = out.rearrange("b (r c j) -> c b r j", r=2, c=G // P)
+        half = TOKENS // NODES
+        nc.sync.dma_start(out=out_view[0], in_=result[0:half, :, :])
+        nc.sync.dma_start(out=out_view[1], in_=result[half : 2 * half, :, :])

@@ -23,11 +23,22 @@ H = 1024
 G = 256
 EPS = 1e-5
 PASSES = H // K_PASS
-TILES = 4
+TILES = 2
 BLOCK = TILES * P
 N_BLOCKS = TOKENS // BLOCK
+LINES = BLOCK // NODES
 CHUNKS = H // P
 HALVES = H // BANK
+CHUNKS_PER_BANK = BANK // BLOCK
+T_BANKS = CHUNKS // CHUNKS_PER_BANK
+G_TILES = G // P
+
+LAG_NORMALISE = 1
+LAG_TRANSPOSE = 2
+LAG_QUANTISE = 3
+LAG_READ_OUT = 4
+X_AHEAD = 2
+LOAD_AHEAD = 4
 
 FLOPS = 2 * TOKENS * H * H + 2 * TOKENS * H * G
 
@@ -47,10 +58,14 @@ def tile_sub_graph_pb_t_kernel(tc, x_nodes, w1, b1, gamma, beta, w2, b2, out):
         const = ctx.enter_context(tc.tile_pool(name="const", bufs=1))
         wstage = ctx.enter_context(tc.tile_pool(name="wstage", bufs=2))
         xpool = ctx.enter_context(tc.tile_pool(name="xpool", bufs=2))
-        hpool = ctx.enter_context(tc.tile_pool(name="hpool", bufs=3))
-        stat = ctx.enter_context(tc.tile_pool(name="stat", bufs=3))
+        hpool = ctx.enter_context(tc.tile_pool(name="hpool", bufs=4))
+        stat = ctx.enter_context(tc.tile_pool(name="stat", bufs=4))
         rpool = ctx.enter_context(tc.tile_pool(name="rpool", bufs=2))
         psum = ctx.enter_context(tc.psum_pool(name="psum", bufs=1))
+        ctx.enter_context(tc.manual_schedule())
+
+        def in_range(blk):
+            return 0 <= blk < N_BLOCKS
 
         w1_raws = {}
         for g in range(PASSES):
@@ -63,27 +78,24 @@ def tile_sub_graph_pb_t_kernel(tc, x_nodes, w1, b1, gamma, beta, w2, b2, out):
                 )
             w1_raws[g] = w1_raw
 
-        x_tiles = {}
+        x_sbs = {}
 
         def load_x(blk):
-            x_sb = xpool.tile([P, TILES * H], BF16, tag="x_sb", bufs=3)
+            if not in_range(blk):
+                return
+            x_sb = xpool.tile([P, TILES * H], BF16, tag="x_sb", bufs=LOAD_AHEAD)
             nc.sync.dma_start(
                 out=x_sb[:].rearrange("p (i k) -> p i k", i=TILES),
                 in_=x[blk * BLOCK : (blk + 1) * BLOCK, :].rearrange("(i p) k -> p i k", p=P),
             )
-            x_tiles[blk] = x_sb
+            x_sbs[blk] = x_sb
 
         load_x(0)
         load_x(1)
         w2_raw = const.tile([P, CHUNKS, G], BF16)
         nc.sync.dma_start(out=w2_raw[:], in_=w2.rearrange("(a p) n -> p a n", p=P))
-
-        ident = const.tile([P, P], F32)
-        make_identity(nc, ident[:])
-        eps_col = const.tile([P, 1], F32)
-        nc.vector.memset(eps_col[:], EPS)
-        warm = const.tile([P, 1], F32)
-        nc.scalar.activation(out=warm[:], in_=eps_col[:], func=ACT.Sqrt)
+        for blk in range(2, LOAD_AHEAD):
+            load_x(blk)
 
         rows = const.tile([P, P], BF16)
         nc.vector.memset(rows[:], 0.0)
@@ -92,23 +104,31 @@ def tile_sub_graph_pb_t_kernel(tc, x_nodes, w1, b1, gamma, beta, w2, b2, out):
             out=rows[CHUNKS : 2 * CHUNKS, :], in_=beta.rearrange("(c p) -> c p", p=P)
         )
         nc.scalar.dma_start(
-            out=rows[2 * CHUNKS : 2 * CHUNKS + 2, :], in_=b2.rearrange("(c p) -> c p", p=P)
+            out=rows[2 * CHUNKS : 2 * CHUNKS + G_TILES, :], in_=b2.rearrange("(c p) -> c p", p=P)
         )
+        b1_row = const.tile([P, H], BF16)
+        nc.vector.memset(b1_row[:], 0.0)
+        nc.scalar.dma_start(out=b1_row[0:1, :], in_=b1.rearrange("(o h) -> o h", o=1))
+
+        ident = const.tile([P, P], F32)
+        make_identity(nc, ident[:])
+        eps_col = const.tile([P, 1], F32)
+        nc.vector.memset(eps_col[:], EPS)
+        ones = const.tile([P, P], BF16)
+        nc.vector.memset(ones[:], 1.0)
+        warm = const.tile([P, 1], F32)
+        nc.scalar.activation(out=warm[:], in_=eps_col[:], func=ACT.Sqrt)
+
         rows_f32 = const.tile([P, P], F32)
         nc.vector.tensor_copy(out=rows_f32[:], in_=rows[:])
         cols_ps = psum.tile([P, P], F32, tag="xT", bufs=2)
         nc.tensor.transpose(cols_ps[:], rows_f32[:], ident[:])
-        cols = const.tile([P, 2 * CHUNKS + 2], F32)
-        nc.vector.tensor_copy(out=cols[:], in_=cols_ps[:, 0 : 2 * CHUNKS + 2])
+        cols = const.tile([P, 2 * CHUNKS + G_TILES], F32)
+        nc.vector.tensor_copy(out=cols[:], in_=cols_ps[:, 0 : 2 * CHUNKS + G_TILES])
         gamma_col = cols[:, 0:CHUNKS]
         beta_col = cols[:, CHUNKS : 2 * CHUNKS]
-        b2_col = cols[:, 2 * CHUNKS : 2 * CHUNKS + 2]
+        b2_col = cols[:, 2 * CHUNKS : 2 * CHUNKS + G_TILES]
 
-        b1_row = const.tile([P, H], BF16)
-        nc.vector.memset(b1_row[:], 0.0)
-        nc.scalar.dma_start(out=b1_row[0:1, :], in_=b1.rearrange("(o h) -> o h", o=1))
-        ones = const.tile([P, P], BF16)
-        nc.vector.memset(ones[:], 1.0)
         b1_all = const.tile([P, H], F32)
         for n in range(HALVES):
             b1_ps = psum.tile([P, BANK], F32, tag="h_ps", bufs=3)
@@ -118,64 +138,52 @@ def tile_sub_graph_pb_t_kernel(tc, x_nodes, w1, b1, gamma, beta, w2, b2, out):
             )
             nc.scalar.copy(out=b1_all[:, n * BANK : (n + 1) * BANK], in_=b1_ps[:])
 
-        w1_codes = const.tile([P, PASSES, H], U32, align_bytes=64)
-        w1_scales = const.tile([P, PASSES, H], U8, align_bytes=64)
-        for g in range(PASSES):
-            for n in range(HALVES):
-                cols_n = slice(n * BANK, (n + 1) * BANK)
-                w1_grp = wstage.tile([P, BANK, PACK], BF16, tag="w1_grp", align_bytes=64)
-                regroup(nc, w1_grp[:], w1_raws[g][:, :, cols_n])
-                nc.vector.quantize_mx(
-                    out=w1_codes[:, g, cols_n].bitcast(FP8X4),
-                    scales=w1_scales[:, g, cols_n],
-                    in_=w1_grp[:].rearrange("p c t -> p (c t)"),
-                )
+        node_max = const.tile([P, G_TILES, TOKENS // NODES], F32)
 
-        w2_grp = const.tile([P, PASSES, G, PACK], BF16, align_bytes=64)
-        w2_codes = const.tile([P, PASSES, G], U32, align_bytes=64)
-        w2_scales = const.tile([P, PASSES, G], U8, align_bytes=64)
-        for g in range(PASSES):
-            regroup(nc, w2_grp[:, g, :, :], w2_raw[:, PACK * g : PACK * (g + 1), :])
-        nc.vector.quantize_mx(
-            out=w2_codes[:].rearrange("p g c -> p (g c)").bitcast(FP8X4),
-            scales=w2_scales[:].rearrange("p g c -> p (g c)"),
-            in_=w2_grp[:].rearrange("p g c t -> p (g c t)"),
-        )
+        x_grps = {}
+        x_mx = {}
 
-        node_max = const.tile([P, 2, TOKENS // NODES], F32)
+        def transpose_x(blk, i):
+            if not in_range(blk):
+                return
+            if i == 0:
+                x_grp = xpool.tile([P, TILES * H], BF16, tag="x_grp", align_bytes=64)
+                x_grps[blk] = x_grp
+            x_words = x_sbs[blk][:].bitcast(F32)
+            x_grp_words = x_grps[blk][:].bitcast(F32)
+            xT_ps = psum.tile([P, PACK, P], F32, tag="xT", bufs=2)
+            for q in range(PACK):
+                w0 = i * (H // 2) + q * P
+                nc.tensor.transpose(xT_ps[:, q, :], x_words[:, w0 : w0 + P], ident[:])
+            nc.scalar.copy(
+                out=x_grp_words[:, i * (H // 2) : (i + 1) * (H // 2)].rearrange(
+                    "p (g w u) -> p g w u", g=PASSES, u=2
+                ),
+                in_=xT_ps[:].rearrange("p (g u) w -> p g w u", g=PASSES),
+            )
 
-        x_quant = {}
-
-        def transpose_and_quantise_x(blk):
-            x_words = x_tiles[blk][:].bitcast(F32)
-            x_grp = xpool.tile([P, TILES * H], BF16, tag="x_grp", align_bytes=64)
-            x_grp_words = x_grp[:].bitcast(F32)
-            for i in range(TILES):
-                xT_ps = psum.tile([P, PACK, P], F32, tag="xT", bufs=2)
-                for q in range(PACK):
-                    w0 = i * (H // 2) + q * P
-                    nc.tensor.transpose(xT_ps[:, q, :], x_words[:, w0 : w0 + P], ident[:])
-                nc.scalar.copy(
-                    out=x_grp_words[:, i * (H // 2) : (i + 1) * (H // 2)].rearrange(
-                        "p (g w u) -> p g w u", g=PASSES, u=2
-                    ),
-                    in_=xT_ps[:].rearrange("p (g u) w -> p g w u", g=PASSES),
-                )
+        def quantise_x(blk):
+            if not in_range(blk):
+                return
             x_codes = xpool.tile([P, TILES, PASSES, P], U32, tag="x_codes", align_bytes=64)
             x_scales = xpool.tile([P, TILES, PASSES, P], U8, tag="x_scales", align_bytes=64)
             nc.vector.quantize_mx(
                 out=x_codes[:].rearrange("p i g w -> p (i g w)").bitcast(FP8X4),
                 scales=x_scales[:].rearrange("p i g w -> p (i g w)"),
-                in_=x_grp[:],
+                in_=x_grps[blk][:],
             )
-            x_quant[blk] = (x_codes, x_scales)
+            x_mx[blk] = (x_codes, x_scales)
 
-        def hidden_layer(blk):
-            x_codes, x_scales = x_quant[blk]
-            h_sb = hpool.tile([P, TILES, H], F32, tag="h_sb")
-            h_sum = stat.tile([P, TILES, HALVES], F32, tag="h_sum")
-            neg_mean = stat.tile([P, TILES], F32, tag="neg_mean")
-            sq_sum = stat.tile([P, TILES], F32, tag="sq_sum")
+        h_pss = {}
+        h_sbs = {}
+        neg_means = {}
+        stds = {}
+        rstds = {}
+
+        def first_matmul(blk):
+            if not in_range(blk):
+                return
+            x_codes, x_scales = x_mx[blk]
             for i in range(TILES):
                 for n in range(HALVES):
                     cols_n = slice(n * BANK, (n + 1) * BANK)
@@ -190,9 +198,20 @@ def tile_sub_graph_pb_t_kernel(tc, x_nodes, w1, b1, gamma, beta, w2, b2, out):
                             start=(g == 0),
                             stop=(g == PASSES - 1),
                         )
+                    h_pss[(blk, i, n)] = h_ps
+
+        def add_bias(blk):
+            if not in_range(blk):
+                return
+            h_sb = hpool.tile([P, TILES, H], F32, tag="h_sb")
+            h_sum = stat.tile([P, TILES, HALVES], F32, tag="h_sum")
+            neg_mean = stat.tile([P, TILES], F32, tag="neg_mean")
+            for i in range(TILES):
+                for n in range(HALVES):
+                    cols_n = slice(n * BANK, (n + 1) * BANK)
                     nc.vector.scalar_tensor_tensor(
                         out=h_sb[:, i, cols_n],
-                        in0=h_ps[:],
+                        in0=h_pss[(blk, i, n)][:],
                         scalar=1.0,
                         in1=b1_all[:, cols_n],
                         op0=ALU.mult,
@@ -207,70 +226,100 @@ def tile_sub_graph_pb_t_kernel(tc, x_nodes, w1, b1, gamma, beta, w2, b2, out):
                     op0=ALU.add,
                     op1=ALU.mult,
                 )
+            h_sbs[blk] = h_sb
+            neg_means[blk] = neg_mean
+
+        def standard_deviation(blk):
+            if not in_range(blk):
+                return
+            sq_sum = stat.tile([P, TILES], F32, tag="sq_sum")
+            for i in range(TILES):
                 squares = hpool.tile([P, H], BF16, tag="squares", bufs=2)
                 nc.scalar.activation(
                     out=squares[:],
-                    in_=h_sb[:, i, :],
+                    in_=h_sbs[blk][:, i, :],
                     func=ACT.Square,
-                    bias=neg_mean[:, i : i + 1],
+                    bias=neg_means[blk][:, i : i + 1],
                     scale=1.0,
                     accum_out=sq_sum[:, i : i + 1],
                 )
-            return h_sb, neg_mean, sq_sum
-
-        def normalise(h_sb, neg_mean, sq_sum):
             std = stat.tile([P, TILES], F32, tag="std")
             nc.scalar.activation(
                 out=std[:], in_=sq_sum[:], func=ACT.Sqrt, bias=eps_col[:, 0:1], scale=1.0 / H
             )
+            stds[blk] = std
+
+        def normalise(blk):
+            if not in_range(blk):
+                return
             rstd = stat.tile([P, TILES], F32, tag="rstd")
-            nc.vector.reciprocal(out=rstd[:], in_=std[:])
+            nc.vector.reciprocal(out=rstd[:], in_=stds[blk][:])
             for i in range(TILES):
                 nc.gpsimd.tensor_scalar(
-                    out=h_sb[:, i, :],
-                    in0=h_sb[:, i, :],
-                    scalar1=neg_mean[:, i : i + 1],
+                    out=h_sbs[blk][:, i, :],
+                    in0=h_sbs[blk][:, i, :],
+                    scalar1=neg_means[blk][:, i : i + 1],
                     scalar2=rstd[:, i : i + 1],
                     op0=ALU.add,
                     op1=ALU.mult,
                 )
 
-        def activate_and_quantise(h_sb):
-            r_planes = rpool.tile([P, CHUNKS, BLOCK], BF16, tag="r_planes")
+        r_planess = {}
+        r_grps = {}
+        r_mx = {}
+
+        def transpose_and_activate(blk, bank):
+            if not in_range(blk):
+                return
+            if bank == 0:
+                r_planes = rpool.tile([P, CHUNKS, BLOCK], BF16, tag="r_planes")
+                r_planess[blk] = r_planes
+            nT_ps = psum.tile([P, CHUNKS_PER_BANK, BLOCK], F32, tag="nT", bufs=2)
+            for s in range(CHUNKS_PER_BANK):
+                c = bank * CHUNKS_PER_BANK + s
+                for i in range(TILES):
+                    nc.tensor.transpose(
+                        nT_ps[:, s, i * P : (i + 1) * P],
+                        h_sbs[blk][:, i, c * P : (c + 1) * P],
+                        ident[:],
+                    )
+            for s in range(CHUNKS_PER_BANK):
+                c = bank * CHUNKS_PER_BANK + s
+                nc.scalar.activation(
+                    out=r_planess[blk][:, c, :],
+                    in_=nT_ps[:, s, :],
+                    func=ACT.Relu,
+                    bias=beta_col[:, c : c + 1],
+                    scale=gamma_col[:, c : c + 1],
+                )
+
+        def quantise_r(blk):
+            if not in_range(blk):
+                return
             r_grp = rpool.tile([P, PASSES, BLOCK, PACK], BF16, tag="r_grp", align_bytes=64)
             r_codes = rpool.tile([P, PASSES, BLOCK], U32, tag="r_codes", align_bytes=64)
             r_scales = rpool.tile([P, PASSES, BLOCK], U8, tag="r_scales", align_bytes=64)
             for g in range(PASSES):
-                for j in range(PACK):
-                    c = PACK * g + j
-                    nT_ps = psum.tile([P, BLOCK], F32, tag="nT", bufs=2)
-                    for i in range(TILES):
-                        nc.tensor.transpose(
-                            nT_ps[:, i * P : (i + 1) * P], h_sb[:, i, c * P : (c + 1) * P], ident[:]
-                        )
-                    nc.scalar.activation(
-                        out=r_planes[:, c, :],
-                        in_=nT_ps[:],
-                        func=ACT.Relu,
-                        bias=beta_col[:, c : c + 1],
-                        scale=gamma_col[:, c : c + 1],
-                    )
-                regroup(nc, r_grp[:, g, :, :], r_planes[:, PACK * g : PACK * (g + 1), :])
+                regroup(nc, r_grp[:, g, :, :], r_planess[blk][:, PACK * g : PACK * (g + 1), :])
             for g in range(PASSES):
                 nc.vector.quantize_mx(
                     out=r_codes[:, g, :].bitcast(FP8X4),
                     scales=r_scales[:, g, :],
                     in_=r_grp[:, g, :, :].rearrange("p w j -> p (w j)"),
                 )
-            return r_codes, r_scales
+            r_mx[blk] = (r_codes, r_scales)
 
-        def read_out(blk, r_codes, r_scales):
-            lines = BLOCK // NODES
-            for cc in range(G // P):
-                x1_ps = psum.tile([P, BLOCK], F32, tag="x1", bufs=1)
+        x1_pss = {}
+
+        def second_matmul(blk):
+            if not in_range(blk):
+                return
+            r_codes, r_scales = r_mx[blk]
+            x1_ps = psum.tile([P, G_TILES, BLOCK], F32, tag="x1", bufs=1)
+            for cc in range(G_TILES):
                 for g in range(PASSES):
                     nc.tensor.matmul_mx(
-                        out=x1_ps[:],
+                        out=x1_ps[:, cc, :],
                         lhsT=w2_codes[:, g, cc * P : (cc + 1) * P].bitcast(FP8X4),
                         lhsT_scale=w2_scales[:, g, cc * P : (cc + 1) * P],
                         rhs=r_codes[:, g, :].bitcast(FP8X4),
@@ -278,25 +327,66 @@ def tile_sub_graph_pb_t_kernel(tc, x_nodes, w1, b1, gamma, beta, w2, b2, out):
                         start=(g == 0),
                         stop=(g == PASSES - 1),
                     )
-                nc.vector.tensor_reduce(
-                    out=node_max[:, cc, blk * lines : (blk + 1) * lines],
-                    in_=x1_ps[:].rearrange("p (q l) -> p q l", l=NODES),
-                    axis=AX.X,
-                    op=ALU.max,
+            x1_pss[blk] = x1_ps
+
+        def node_maxima(blk):
+            if not in_range(blk):
+                return
+            nc.vector.tensor_reduce(
+                out=node_max[:, :, blk * LINES : (blk + 1) * LINES],
+                in_=x1_pss[blk][:].rearrange("p c (q l) -> p c q l", l=NODES),
+                axis=AX.X,
+                op=ALU.max,
+            )
+
+        for blk in range(X_AHEAD):
+            for i in range(TILES):
+                transpose_x(blk, i)
+
+        w1_codes = const.tile([P, PASSES, H], U32, align_bytes=64)
+        w1_scales = const.tile([P, PASSES, H], U8, align_bytes=64)
+        for g in range(PASSES):
+            w1_grps = {}
+            for n in range(HALVES):
+                w1_grp = wstage.tile([P, BANK, PACK], BF16, tag="w1_grp", align_bytes=64)
+                regroup(nc, w1_grp[:], w1_raws[g][:, :, n * BANK : (n + 1) * BANK])
+                w1_grps[n] = w1_grp
+            for n in range(HALVES):
+                cols_n = slice(n * BANK, (n + 1) * BANK)
+                nc.vector.quantize_mx(
+                    out=w1_codes[:, g, cols_n].bitcast(FP8X4),
+                    scales=w1_scales[:, g, cols_n],
+                    in_=w1_grps[n][:].rearrange("p c t -> p (c t)"),
                 )
+        quantise_x(0)
 
-        transpose_and_quantise_x(0)
-        for blk in range(N_BLOCKS):
-            if blk + 2 < N_BLOCKS:
-                load_x(blk + 2)
-            if blk + 1 < N_BLOCKS:
-                transpose_and_quantise_x(blk + 1)
-            h_sb, neg_mean, sq_sum = hidden_layer(blk)
-            normalise(h_sb, neg_mean, sq_sum)
-            r_codes, r_scales = activate_and_quantise(h_sb)
-            read_out(blk, r_codes, r_scales)
+        w2_grp = const.tile([P, PASSES, G, PACK], BF16, align_bytes=64)
+        w2_codes = const.tile([P, PASSES, G], U32, align_bytes=64)
+        w2_scales = const.tile([P, PASSES, G], U8, align_bytes=64)
+        for g in range(PASSES):
+            regroup(nc, w2_grp[:, g, :, :], w2_raw[:, PACK * g : PACK * (g + 1), :])
+        nc.vector.quantize_mx(
+            out=w2_codes[:].rearrange("p g c -> p (g c)").bitcast(FP8X4),
+            scales=w2_scales[:].rearrange("p g c -> p (g c)"),
+            in_=w2_grp[:].rearrange("p g c t -> p (g c t)"),
+        )
 
-        for cc in range(G // P):
+        for step in range(N_BLOCKS + LAG_READ_OUT):
+            load_x(step + LOAD_AHEAD)
+            quantise_x(step + 1)
+            quantise_r(step - LAG_QUANTISE)
+            normalise(step - LAG_NORMALISE)
+            first_matmul(step)
+            second_matmul(step - LAG_READ_OUT)
+            add_bias(step)
+            node_maxima(step - LAG_READ_OUT)
+            for bank in range(T_BANKS):
+                transpose_and_activate(step - LAG_TRANSPOSE, bank)
+                if (bank + 1) % (T_BANKS // TILES) == 0:
+                    transpose_x(step + X_AHEAD, bank // (T_BANKS // TILES))
+            standard_deviation(step)
+
+        for cc in range(G_TILES):
             nc.vector.tensor_scalar_add(
                 out=node_max[:, cc, :], in0=node_max[:, cc, :], scalar1=b2_col[:, cc : cc + 1]
             )
@@ -305,7 +395,9 @@ def tile_sub_graph_pb_t_kernel(tc, x_nodes, w1, b1, gamma, beta, w2, b2, out):
         result = const.tile([P, 2, P], F32)
         for rep in range(2):
             nc.vector.tensor_copy(out=result[:, rep, :], in_=maxT_ps[:])
-        out_view = out.rearrange("b (r c j) -> c b r j", r=2, c=G // P)
-        half = TOKENS // NODES
-        nc.sync.dma_start(out=out_view[0], in_=result[0:half, :, :])
-        nc.sync.dma_start(out=out_view[1], in_=result[half : 2 * half, :, :])
+        out_view = out.rearrange("b (r c j) -> c b r j", r=2, c=G_TILES)
+        n_lines = TOKENS // NODES
+        for cc in range(G_TILES):
+            nc.sync.dma_start(
+                out=out_view[cc], in_=result[cc * n_lines : (cc + 1) * n_lines, :, :]
+            )

@@ -33,9 +33,9 @@ CHUNKS_PER_BANK = BANK // BLOCK
 T_BANKS = CHUNKS // CHUNKS_PER_BANK
 G_TILES = G // P
 
-LAG_NORMALISE = 1
-LAG_TRANSPOSE = 2
-LAG_QUANTISE = 3
+LAG_DEVIATION = 1
+LAG_NORMALISE = 2
+LAG_TRANSPOSE = 3
 LAG_READ_OUT = 4
 X_AHEAD = 2
 LOAD_AHEAD = 4
@@ -58,7 +58,7 @@ def tile_sub_graph_pb_t_kernel(tc, x_nodes, w1, b1, gamma, beta, w2, b2, out):
         const = ctx.enter_context(tc.tile_pool(name="const", bufs=1))
         wstage = ctx.enter_context(tc.tile_pool(name="wstage", bufs=2))
         xpool = ctx.enter_context(tc.tile_pool(name="xpool", bufs=2))
-        hpool = ctx.enter_context(tc.tile_pool(name="hpool", bufs=4))
+        hpool = ctx.enter_context(tc.tile_pool(name="hpool", bufs=5))
         stat = ctx.enter_context(tc.tile_pool(name="stat", bufs=4))
         rpool = ctx.enter_context(tc.tile_pool(name="rpool", bufs=2))
         psum = ctx.enter_context(tc.psum_pool(name="psum", bufs=1))
@@ -121,7 +121,7 @@ def tile_sub_graph_pb_t_kernel(tc, x_nodes, w1, b1, gamma, beta, w2, b2, out):
 
         rows_f32 = const.tile([P, P], F32)
         nc.vector.tensor_copy(out=rows_f32[:], in_=rows[:])
-        cols_ps = psum.tile([P, P], F32, tag="xT", bufs=2)
+        cols_ps = psum.tile([P, P], F32, tag="xT", bufs=1)
         nc.tensor.transpose(cols_ps[:], rows_f32[:], ident[:])
         cols = const.tile([P, 2 * CHUNKS + G_TILES], F32)
         nc.vector.tensor_copy(out=cols[:], in_=cols_ps[:, 0 : 2 * CHUNKS + G_TILES])
@@ -131,7 +131,7 @@ def tile_sub_graph_pb_t_kernel(tc, x_nodes, w1, b1, gamma, beta, w2, b2, out):
 
         b1_all = const.tile([P, H], F32)
         for n in range(HALVES):
-            b1_ps = psum.tile([P, BANK], F32, tag="h_ps", bufs=3)
+            b1_ps = psum.tile([P, BANK], F32, tag="h_ps", bufs=4)
             nc.tensor.matmul(
                 out=b1_ps[:], lhsT=ones[:], rhs=b1_row[:, n * BANK : (n + 1) * BANK],
                 start=True, stop=True,
@@ -151,7 +151,7 @@ def tile_sub_graph_pb_t_kernel(tc, x_nodes, w1, b1, gamma, beta, w2, b2, out):
                 x_grps[blk] = x_grp
             x_words = x_sbs[blk][:].bitcast(F32)
             x_grp_words = x_grps[blk][:].bitcast(F32)
-            xT_ps = psum.tile([P, PACK, P], F32, tag="xT", bufs=2)
+            xT_ps = psum.tile([P, PACK, P], F32, tag="xT", bufs=1)
             for q in range(PACK):
                 w0 = i * (H // 2) + q * P
                 nc.tensor.transpose(xT_ps[:, q, :], x_words[:, w0 : w0 + P], ident[:])
@@ -177,28 +177,26 @@ def tile_sub_graph_pb_t_kernel(tc, x_nodes, w1, b1, gamma, beta, w2, b2, out):
         h_pss = {}
         h_sbs = {}
         neg_means = {}
+        sq_sums = {}
         stds = {}
-        rstds = {}
 
-        def first_matmul(blk):
+        def first_matmul(blk, i, n):
             if not in_range(blk):
                 return
             x_codes, x_scales = x_mx[blk]
-            for i in range(TILES):
-                for n in range(HALVES):
-                    cols_n = slice(n * BANK, (n + 1) * BANK)
-                    h_ps = psum.tile([P, BANK], F32, tag="h_ps", bufs=3)
-                    for g in range(PASSES):
-                        nc.tensor.matmul_mx(
-                            out=h_ps[:],
-                            lhsT=x_codes[:, i, g, :].bitcast(FP8X4),
-                            lhsT_scale=x_scales[:, i, g, :],
-                            rhs=w1_codes[:, g, cols_n].bitcast(FP8X4),
-                            rhs_scale=w1_scales[:, g, cols_n],
-                            start=(g == 0),
-                            stop=(g == PASSES - 1),
-                        )
-                    h_pss[(blk, i, n)] = h_ps
+            cols_n = slice(n * BANK, (n + 1) * BANK)
+            h_ps = psum.tile([P, BANK], F32, tag="h_ps", bufs=4)
+            for g in range(PASSES):
+                nc.tensor.matmul_mx(
+                    out=h_ps[:],
+                    lhsT=x_codes[:, i, g, :].bitcast(FP8X4),
+                    lhsT_scale=x_scales[:, i, g, :],
+                    rhs=w1_codes[:, g, cols_n].bitcast(FP8X4),
+                    rhs_scale=w1_scales[:, g, cols_n],
+                    start=(g == 0),
+                    stop=(g == PASSES - 1),
+                )
+            h_pss[(blk, i, n)] = h_ps
 
         def add_bias(blk):
             if not in_range(blk):
@@ -229,23 +227,29 @@ def tile_sub_graph_pb_t_kernel(tc, x_nodes, w1, b1, gamma, beta, w2, b2, out):
             h_sbs[blk] = h_sb
             neg_means[blk] = neg_mean
 
+        def squared_deviations(blk, i):
+            if not in_range(blk):
+                return
+            if i == 0:
+                sq_sum = stat.tile([P, TILES], F32, tag="sq_sum")
+                sq_sums[blk] = sq_sum
+            squares = hpool.tile([P, H], BF16, tag="squares", bufs=2)
+            nc.scalar.activation(
+                out=squares[:],
+                in_=h_sbs[blk][:, i, :],
+                func=ACT.Square,
+                bias=neg_means[blk][:, i : i + 1],
+                scale=1.0,
+                accum_out=sq_sums[blk][:, i : i + 1],
+            )
+
         def standard_deviation(blk):
             if not in_range(blk):
                 return
-            sq_sum = stat.tile([P, TILES], F32, tag="sq_sum")
-            for i in range(TILES):
-                squares = hpool.tile([P, H], BF16, tag="squares", bufs=2)
-                nc.scalar.activation(
-                    out=squares[:],
-                    in_=h_sbs[blk][:, i, :],
-                    func=ACT.Square,
-                    bias=neg_means[blk][:, i : i + 1],
-                    scale=1.0,
-                    accum_out=sq_sum[:, i : i + 1],
-                )
             std = stat.tile([P, TILES], F32, tag="std")
             nc.scalar.activation(
-                out=std[:], in_=sq_sum[:], func=ACT.Sqrt, bias=eps_col[:, 0:1], scale=1.0 / H
+                out=std[:], in_=sq_sums[blk][:], func=ACT.Sqrt, bias=eps_col[:, 0:1],
+                scale=1.0 / H,
             )
             stds[blk] = std
 
@@ -374,23 +378,26 @@ def tile_sub_graph_pb_t_kernel(tc, x_nodes, w1, b1, gamma, beta, w2, b2, out):
         for step in range(N_BLOCKS + LAG_READ_OUT):
             load_x(step + LOAD_AHEAD)
             quantise_x(step + 1)
-            quantise_r(step - LAG_QUANTISE)
+            quantise_r(step - LAG_READ_OUT)
             normalise(step - LAG_NORMALISE)
-            first_matmul(step)
+            for i in range(TILES):
+                for n in range(HALVES):
+                    first_matmul(step, i, n)
+                    if n == 0:
+                        squared_deviations(step - LAG_DEVIATION, i)
+                    transpose_and_activate(step - LAG_TRANSPOSE, i * HALVES + n)
+                    if n == HALVES - 1:
+                        transpose_x(step + X_AHEAD, i)
             second_matmul(step - LAG_READ_OUT)
+            standard_deviation(step - LAG_DEVIATION)
             add_bias(step)
             node_maxima(step - LAG_READ_OUT)
-            for bank in range(T_BANKS):
-                transpose_and_activate(step - LAG_TRANSPOSE, bank)
-                if (bank + 1) % (T_BANKS // TILES) == 0:
-                    transpose_x(step + X_AHEAD, bank // (T_BANKS // TILES))
-            standard_deviation(step)
 
         for cc in range(G_TILES):
             nc.vector.tensor_scalar_add(
                 out=node_max[:, cc, :], in0=node_max[:, cc, :], scalar1=b2_col[:, cc : cc + 1]
             )
-        maxT_ps = psum.tile([P, P], F32, tag="xT", bufs=2)
+        maxT_ps = psum.tile([P, P], F32, tag="xT", bufs=1)
         nc.tensor.transpose(maxT_ps[:], node_max[:].rearrange("p c b -> p (c b)"), ident[:])
         result = const.tile([P, 2, P], F32)
         for rep in range(2):

@@ -383,11 +383,10 @@ def tile_sub_graph_pb_t_kernel(tc, x_nodes, w1, b1, gamma, beta, w2, b2, out):
             for i in range(TILES):
                 for n in range(HALVES):
                     first_matmul(step, i, n)
-                    if n == 0:
-                        squared_deviations(step - LAG_DEVIATION, i)
+                squared_deviations(step - LAG_DEVIATION, i)
+                for n in range(HALVES):
                     transpose_and_activate(step - LAG_TRANSPOSE, i * HALVES + n)
-                    if n == HALVES - 1:
-                        transpose_x(step + X_AHEAD, i)
+                transpose_x(step + X_AHEAD, i)
             second_matmul(step - LAG_READ_OUT)
             standard_deviation(step - LAG_DEVIATION)
             add_bias(step)

@@ -141,6 +141,7 @@ def tile_sub_graph_pb_t_kernel(tc, x_nodes, w1, b1, gamma, beta, w2, b2, out):
         node_max = const.tile([P, G_TILES, TOKENS // NODES], F32)
 
         x_grps = {}
+        xT_pss = {}
         x_mx = {}
 
         def transpose_x(blk, i):
@@ -150,16 +151,21 @@ def tile_sub_graph_pb_t_kernel(tc, x_nodes, w1, b1, gamma, beta, w2, b2, out):
                 x_grp = xpool.tile([P, TILES * H], BF16, tag="x_grp", align_bytes=64)
                 x_grps[blk] = x_grp
             x_words = x_sbs[blk][:].bitcast(F32)
-            x_grp_words = x_grps[blk][:].bitcast(F32)
             xT_ps = psum.tile([P, PACK, P], F32, tag="xT", bufs=1)
             for q in range(PACK):
                 w0 = i * (H // 2) + q * P
                 nc.tensor.transpose(xT_ps[:, q, :], x_words[:, w0 : w0 + P], ident[:])
-            nc.scalar.copy(
+            xT_pss[(blk, i)] = xT_ps
+
+        def copy_x(copy, blk, i):
+            if not in_range(blk):
+                return
+            x_grp_words = x_grps[blk][:].bitcast(F32)
+            copy(
                 out=x_grp_words[:, i * (H // 2) : (i + 1) * (H // 2)].rearrange(
                     "p (g w u) -> p g w u", g=PASSES, u=2
                 ),
-                in_=xT_ps[:].rearrange("p (g u) w -> p g w u", g=PASSES),
+                in_=xT_pss[(blk, i)][:].rearrange("p (g u) w -> p g w u", g=PASSES),
             )
 
         def quantise_x(blk):
@@ -216,7 +222,7 @@ def tile_sub_graph_pb_t_kernel(tc, x_nodes, w1, b1, gamma, beta, w2, b2, out):
                         op1=ALU.add,
                         accum_out=h_sum[:, i, n : n + 1],
                     )
-                nc.vector.tensor_scalar(
+                nc.gpsimd.tensor_scalar(
                     out=neg_mean[:, i : i + 1],
                     in0=h_sum[:, i, 0:1],
                     scalar1=h_sum[:, i, 1:2],
@@ -297,20 +303,26 @@ def tile_sub_graph_pb_t_kernel(tc, x_nodes, w1, b1, gamma, beta, w2, b2, out):
                     scale=gamma_col[:, c : c + 1],
                 )
 
-        def quantise_r(blk):
+        def regroup_r(blk):
             if not in_range(blk):
                 return
             r_grp = rpool.tile([P, PASSES, BLOCK, PACK], BF16, tag="r_grp", align_bytes=64)
+            nc.vector.tensor_copy(
+                out=r_grp[:].rearrange("p g (c i) t -> p g c t i", i=4),
+                in_=r_planess[blk][:].rearrange("p (g t) (c i) -> p g c t i", g=PASSES, i=4),
+            )
+            r_grps[blk] = r_grp
+
+        def quantise_r(blk):
+            if not in_range(blk):
+                return
             r_codes = rpool.tile([P, PASSES, BLOCK], U32, tag="r_codes", align_bytes=64)
             r_scales = rpool.tile([P, PASSES, BLOCK], U8, tag="r_scales", align_bytes=64)
-            for g in range(PASSES):
-                regroup(nc, r_grp[:, g, :, :], r_planess[blk][:, PACK * g : PACK * (g + 1), :])
-            for g in range(PASSES):
-                nc.vector.quantize_mx(
-                    out=r_codes[:, g, :].bitcast(FP8X4),
-                    scales=r_scales[:, g, :],
-                    in_=r_grp[:, g, :, :].rearrange("p w j -> p (w j)"),
-                )
+            nc.vector.quantize_mx(
+                out=r_codes[:].rearrange("p g w -> p (g w)").bitcast(FP8X4),
+                scales=r_scales[:].rearrange("p g w -> p (g w)"),
+                in_=r_grps[blk][:].rearrange("p g w j -> p (g w j)"),
+            )
             r_mx[blk] = (r_codes, r_scales)
 
         x1_pss = {}
@@ -346,6 +358,7 @@ def tile_sub_graph_pb_t_kernel(tc, x_nodes, w1, b1, gamma, beta, w2, b2, out):
         for blk in range(X_AHEAD):
             for i in range(TILES):
                 transpose_x(blk, i)
+                copy_x(nc.scalar.copy, blk, i)
 
         w1_codes = const.tile([P, PASSES, H], U32, align_bytes=64)
         w1_scales = const.tile([P, PASSES, H], U8, align_bytes=64)
@@ -377,6 +390,7 @@ def tile_sub_graph_pb_t_kernel(tc, x_nodes, w1, b1, gamma, beta, w2, b2, out):
 
         for step in range(N_BLOCKS + LAG_READ_OUT):
             load_x(step + LOAD_AHEAD)
+            regroup_r(step - LAG_READ_OUT)
             quantise_x(step + 1)
             quantise_r(step - LAG_READ_OUT)
             normalise(step - LAG_NORMALISE)
@@ -387,9 +401,12 @@ def tile_sub_graph_pb_t_kernel(tc, x_nodes, w1, b1, gamma, beta, w2, b2, out):
                 for n in range(HALVES):
                     transpose_and_activate(step - LAG_TRANSPOSE, i * HALVES + n)
                 transpose_x(step + X_AHEAD, i)
+                if i < TILES - 1:
+                    copy_x(nc.scalar.copy, step + X_AHEAD, i)
             second_matmul(step - LAG_READ_OUT)
             standard_deviation(step - LAG_DEVIATION)
             add_bias(step)
+            copy_x(nc.vector.tensor_copy, step + X_AHEAD, TILES - 1)
             node_maxima(step - LAG_READ_OUT)
 
         for cc in range(G_TILES):

from contextlib import ExitStack

import concourse.mybir as mybir
from concourse.masks import make_identity

F32 = mybir.dt.float32
BF16 = mybir.dt.bfloat16
U32 = mybir.dt.uint32
U8 = mybir.dt.uint8
FP8X4 = mybir.dt.float8_e4m3fn_x4
ACT = mybir.ActivationFunctionType
ALU = mybir.AluOpType
AX = mybir.AxisListType

P = 128
PACK = 4
K_PASS = P * PACK
BANK = 512

TOKENS = 64 * 64
NODES = 64
H = 1024
G = 256
EPS = 1e-5
PASSES = H // K_PASS
TILES = 2
BLOCK = TILES * P
N_BLOCKS = TOKENS // BLOCK
LINES = BLOCK // NODES
CHUNKS = H // P
HALVES = H // BANK
CHUNKS_PER_BANK = BANK // BLOCK
T_BANKS = CHUNKS // CHUNKS_PER_BANK
G_TILES = G // P

LAG_DEVIATION = 1
LAG_NORMALISE = 2
LAG_TRANSPOSE = 3
LAG_READ_OUT = 4
X_AHEAD = 2
LOAD_AHEAD = 4

FLOPS = 2 * TOKENS * H * H + 2 * TOKENS * H * G


def regroup(nc, grouped, planes):
    nc.vector.tensor_copy(
        out=grouped.rearrange("p (c i) t -> p c t i", i=4),
        in_=planes.rearrange("p t (c i) -> p c t i", i=4),
    )


def tile_sub_graph_pb_t_kernel(tc, x_nodes, w1, b1, gamma, beta, w2, b2, out):
    nc = tc.nc
    x = x_nodes.rearrange("b l k -> (b l) k")

    with ExitStack() as ctx:
        const = ctx.enter_context(tc.tile_pool(name="const", bufs=1))
        wstage = ctx.enter_context(tc.tile_pool(name="wstage", bufs=2))
        xpool = ctx.enter_context(tc.tile_pool(name="xpool", bufs=2))
        hpool = ctx.enter_context(tc.tile_pool(name="hpool", bufs=5))
        stat = ctx.enter_context(tc.tile_pool(name="stat", bufs=4))
        rpool = ctx.enter_context(tc.tile_pool(name="rpool", bufs=2))
        psum = ctx.enter_context(tc.psum_pool(name="psum", bufs=1))
        ctx.enter_context(tc.manual_schedule())

        def in_range(blk):
            return 0 <= blk < N_BLOCKS

        w1_raws = {}
        for g in range(PASSES):
            w1_raw = wstage.tile([P, PACK, H], BF16, tag="w1_raw")
            for u in range(2):
                k0 = K_PASS * g + 256 * u
                nc.sync.dma_start(
                    out=w1_raw[:, 2 * u : 2 * u + 2, :],
                    in_=w1[k0 : k0 + 256, :].rearrange("(p e) c -> p e c", e=2),
                )
            w1_raws[g] = w1_raw

        x_sbs = {}

        def load_x(blk):
            if not in_range(blk):
                return
            x_sb = xpool.tile([P, TILES * H], BF16, tag="x_sb", bufs=LOAD_AHEAD)
            nc.sync.dma_start(
                out=x_sb[:].rearrange("p (i k) -> p i k", i=TILES),
                in_=x[blk * BLOCK : (blk + 1) * BLOCK, :].rearrange("(i p) k -> p i k", p=P),
            )
            x_sbs[blk] = x_sb

        load_x(0)
        load_x(1)
        w2_raw = const.tile([P, CHUNKS, G], BF16)
        nc.sync.dma_start(out=w2_raw[:], in_=w2.rearrange("(a p) n -> p a n", p=P))
        for blk in range(2, LOAD_AHEAD):
            load_x(blk)

        rows = const.tile([P, P], BF16)
        nc.vector.memset(rows[:], 0.0)
        nc.scalar.dma_start(out=rows[0:CHUNKS, :], in_=gamma.rearrange("(c p) -> c p", p=P))
        nc.scalar.dma_start(
            out=rows[CHUNKS : 2 * CHUNKS, :], in_=beta.rearrange("(c p) -> c p", p=P)
        )
        nc.scalar.dma_start(
            out=rows[2 * CHUNKS : 2 * CHUNKS + G_TILES, :], in_=b2.rearrange("(c p) -> c p", p=P)
        )
        b1_row = const.tile([P, H], BF16)
        nc.vector.memset(b1_row[:], 0.0)
        nc.scalar.dma_start(out=b1_row[0:1, :], in_=b1.rearrange("(o h) -> o h", o=1))

        ident = const.tile([P, P], F32)
        make_identity(nc, ident[:])
        eps_col = const.tile([P, 1], F32)
        nc.vector.memset(eps_col[:], EPS)
        ones = const.tile([P, P], BF16)
        nc.vector.memset(ones[:], 1.0)
        warm = const.tile([P, 1], F32)
        nc.scalar.activation(out=warm[:], in_=eps_col[:], func=ACT.Sqrt)

        rows_f32 = const.tile([P, P], F32)
        nc.vector.tensor_copy(out=rows_f32[:], in_=rows[:])
        cols_ps = psum.tile([P, P], F32, tag="xT", bufs=1)
        nc.tensor.transpose(cols_ps[:], rows_f32[:], ident[:])
        cols = const.tile([P, 2 * CHUNKS + G_TILES], F32)
        nc.vector.tensor_copy(out=cols[:], in_=cols_ps[:, 0 : 2 * CHUNKS + G_TILES])
        gamma_col = cols[:, 0:CHUNKS]
        beta_col = cols[:, CHUNKS : 2 * CHUNKS]
        b2_col = cols[:, 2 * CHUNKS : 2 * CHUNKS + G_TILES]

        b1_all = const.tile([P, H], F32)
        for n in range(HALVES):
            b1_ps = psum.tile([P, BANK], F32, tag="h_ps", bufs=4)
            nc.tensor.matmul(
                out=b1_ps[:], lhsT=ones[:], rhs=b1_row[:, n * BANK : (n + 1) * BANK],
                start=True, stop=True,
            )
            nc.scalar.copy(out=b1_all[:, n * BANK : (n + 1) * BANK], in_=b1_ps[:])

        node_max = const.tile([P, G_TILES, TOKENS // NODES], F32)

        x_grps = {}
        xT_pss = {}
        x_mx = {}

        def transpose_x(blk, i):
            if not in_range(blk):
                return
            if i == 0:
                x_grp = xpool.tile([P, TILES * H], BF16, tag="x_grp", align_bytes=64)
                x_grps[blk] = x_grp
            x_words = x_sbs[blk][:].bitcast(F32)
            xT_ps = psum.tile([P, PACK, P], F32, tag="xT", bufs=1)
            for q in range(PACK):
                w0 = i * (H // 2) + q * P
                nc.tensor.transpose(xT_ps[:, q, :], x_words[:, w0 : w0 + P], ident[:])
            xT_pss[(blk, i)] = xT_ps

        def copy_x(copy, blk, i):
            if not in_range(blk):
                return
            x_grp_words = x_grps[blk][:].bitcast(F32)
            copy(
                out=x_grp_words[:, i * (H // 2) : (i + 1) * (H // 2)].rearrange(
                    "p (g w u) -> p g w u", g=PASSES, u=2
                ),
                in_=xT_pss[(blk, i)][:].rearrange("p (g u) w -> p g w u", g=PASSES),
            )

        def quantise_x(blk):
            if not in_range(blk):
                return
            x_codes = xpool.tile([P, TILES, PASSES, P], U32, tag="x_codes", align_bytes=64)
            x_scales = xpool.tile([P, TILES, PASSES, P], U8, tag="x_scales", align_bytes=64)
            nc.vector.quantize_mx(
                out=x_codes[:].rearrange("p i g w -> p (i g w)").bitcast(FP8X4),
                scales=x_scales[:].rearrange("p i g w -> p (i g w)"),
                in_=x_grps[blk][:],
            )
            x_mx[blk] = (x_codes, x_scales)

        h_pss = {}
        h_sbs = {}
        neg_means = {}
        sq_sums = {}
        stds = {}

        def first_matmul(blk, i, n):
            if not in_range(blk):
                return
            x_codes, x_scales = x_mx[blk]
            cols_n = slice(n * BANK, (n + 1) * BANK)
            h_ps = psum.tile([P, BANK], F32, tag="h_ps", bufs=4)
            for g in range(PASSES):
                nc.tensor.matmul_mx(
                    out=h_ps[:],
                    lhsT=x_codes[:, i, g, :].bitcast(FP8X4),
                    lhsT_scale=x_scales[:, i, g, :],
                    rhs=w1_codes[:, g, cols_n].bitcast(FP8X4),
                    rhs_scale=w1_scales[:, g, cols_n],
                    start=(g == 0),
                    stop=(g == PASSES - 1),
                )
            h_pss[(blk, i, n)] = h_ps

        def add_bias(blk):
            if not in_range(blk):
                return
            h_sb = hpool.tile([P, TILES, H], F32, tag="h_sb")
            h_sum = stat.tile([P, TILES, HALVES], F32, tag="h_sum")
            neg_mean = stat.tile([P, TILES], F32, tag="neg_mean")
            for i in range(TILES):
                for n in range(HALVES):
                    cols_n = slice(n * BANK, (n + 1) * BANK)
                    nc.vector.scalar_tensor_tensor(
                        out=h_sb[:, i, cols_n],
                        in0=h_pss[(blk, i, n)][:],
                        scalar=1.0,
                        in1=b1_all[:, cols_n],
                        op0=ALU.mult,
                        op1=ALU.add,
                        accum_out=h_sum[:, i, n : n + 1],
                    )
                nc.gpsimd.tensor_scalar(
                    out=neg_mean[:, i : i + 1],
                    in0=h_sum[:, i, 0:1],
                    scalar1=h_sum[:, i, 1:2],
                    scalar2=-1.0 / H,
                    op0=ALU.add,
                    op1=ALU.mult,
                )
            h_sbs[blk] = h_sb
            neg_means[blk] = neg_mean

        def squared_deviations(blk, i):
            if not in_range(blk):
                return
            if i == 0:
                sq_sum = stat.tile([P, TILES], F32, tag="sq_sum")
                sq_sums[blk] = sq_sum
            squares = hpool.tile([P, H], BF16, tag="squares", bufs=2)
            nc.scalar.activation(
                out=squares[:],
                in_=h_sbs[blk][:, i, :],
                func=ACT.Square,
                bias=neg_means[blk][:, i : i + 1],
                scale=1.0,
                accum_out=sq_sums[blk][:, i : i + 1],
            )

        def standard_deviation(blk):
            if not in_range(blk):
                return
            std = stat.tile([P, TILES], F32, tag="std")
            nc.scalar.activation(
                out=std[:], in_=sq_sums[blk][:], func=ACT.Sqrt, bias=eps_col[:, 0:1],
                scale=1.0 / H,
            )
            stds[blk] = std

        def normalise(blk):
            if not in_range(blk):
                return
            rstd = stat.tile([P, TILES], F32, tag="rstd")
            nc.vector.reciprocal(out=rstd[:], in_=stds[blk][:])
            for i in range(TILES):
                nc.gpsimd.tensor_scalar(
                    out=h_sbs[blk][:, i, :],
                    in0=h_sbs[blk][:, i, :],
                    scalar1=neg_means[blk][:, i : i + 1],
                    scalar2=rstd[:, i : i + 1],
                    op0=ALU.add,
                    op1=ALU.mult,
                )

        r_planess = {}
        r_grps = {}
        r_mx = {}

        def transpose_and_activate(blk, bank):
            if not in_range(blk):
                return
            if bank == 0:
                r_planes = rpool.tile([P, CHUNKS, BLOCK], BF16, tag="r_planes")
                r_planess[blk] = r_planes
            nT_ps = psum.tile([P, CHUNKS_PER_BANK, BLOCK], F32, tag="nT", bufs=2)
            for s in range(CHUNKS_PER_BANK):
                c = bank * CHUNKS_PER_BANK + s
                for i in range(TILES):
                    nc.tensor.transpose(
                        nT_ps[:, s, i * P : (i + 1) * P],
                        h_sbs[blk][:, i, c * P : (c + 1) * P],
                        ident[:],
                    )
            for s in range(CHUNKS_PER_BANK):
                c = bank * CHUNKS_PER_BANK + s
                nc.scalar.activation(
                    out=r_planess[blk][:, c, :],
                    in_=nT_ps[:, s, :],
                    func=ACT.Relu,
                    bias=beta_col[:, c : c + 1],
                    scale=gamma_col[:, c : c + 1],
                )

        def regroup_r(blk):
            if not in_range(blk):
                return
            r_grp = rpool.tile([P, PASSES, BLOCK, PACK], BF16, tag="r_grp", align_bytes=64)
            nc.vector.tensor_copy(
                out=r_grp[:].rearrange("p g (c i) t -> p g c t i", i=4),
                in_=r_planess[blk][:].rearrange("p (g t) (c i) -> p g c t i", g=PASSES, i=4),
            )
            r_grps[blk] = r_grp

        def quantise_r(blk):
            if not in_range(blk):
                return
            r_codes = rpool.tile([P, PASSES, BLOCK], U32, tag="r_codes", align_bytes=64)
            r_scales = rpool.tile([P, PASSES, BLOCK], U8, tag="r_scales", align_bytes=64)
            nc.vector.quantize_mx(
                out=r_codes[:].rearrange("p g w -> p (g w)").bitcast(FP8X4),
                scales=r_scales[:].rearrange("p g w -> p (g w)"),
                in_=r_grps[blk][:].rearrange("p g w j -> p (g w j)"),
            )
            r_mx[blk] = (r_codes, r_scales)

        x1_pss = {}

        def second_matmul(blk):
            if not in_range(blk):
                return
            r_codes, r_scales = r_mx[blk]
            x1_ps = psum.tile([P, G_TILES, BLOCK], F32, tag="x1", bufs=1)
            for cc in range(G_TILES):
                for g in range(PASSES):
                    nc.tensor.matmul_mx(
                        out=x1_ps[:, cc, :],
                        lhsT=w2_codes[:, g, cc * P : (cc + 1) * P].bitcast(FP8X4),
                        lhsT_scale=w2_scales[:, g, cc * P : (cc + 1) * P],
                        rhs=r_codes[:, g, :].bitcast(FP8X4),
                        rhs_scale=r_scales[:, g, :],
                        start=(g == 0),
                        stop=(g == PASSES - 1),
                    )
            x1_pss[blk] = x1_ps

        def node_maxima(blk):
            if not in_range(blk):
                return
            nc.vector.tensor_reduce(
                out=node_max[:, :, blk * LINES : (blk + 1) * LINES],
                in_=x1_pss[blk][:].rearrange("p c (q l) -> p c q l", l=NODES),
                axis=AX.X,
                op=ALU.max,
            )

        for blk in range(X_AHEAD):
            for i in range(TILES):
                transpose_x(blk, i)
                copy_x(nc.scalar.copy, blk, i)

        w1_codes = const.tile([P, PASSES, H], U32, align_bytes=64)
        w1_scales = const.tile([P, PASSES, H], U8, align_bytes=64)
        for g in range(PASSES):
            w1_grps = {}
            for n in range(HALVES):
                w1_grp = wstage.tile([P, BANK, PACK], BF16, tag="w1_grp", align_bytes=64)
                regroup(nc, w1_grp[:], w1_raws[g][:, :, n * BANK : (n + 1) * BANK])
                w1_grps[n] = w1_grp
            for n in range(HALVES):
                cols_n = slice(n * BANK, (n + 1) * BANK)
                nc.vector.quantize_mx(
                    out=w1_codes[:, g, cols_n].bitcast(FP8X4),
                    scales=w1_scales[:, g, cols_n],
                    in_=w1_grps[n][:].rearrange("p c t -> p (c t)"),
                )
        quantise_x(0)

        w2_grp = const.tile([P, PASSES, G, PACK], BF16, align_bytes=64)
        w2_codes = const.tile([P, PASSES, G], U32, align_bytes=64)
        w2_scales = const.tile([P, PASSES, G], U8, align_bytes=64)
        for g in range(PASSES):
            regroup(nc, w2_grp[:, g, :, :], w2_raw[:, PACK * g : PACK * (g + 1), :])
        nc.vector.quantize_mx(
            out=w2_codes[:].rearrange("p g c -> p (g c)").bitcast(FP8X4),
            scales=w2_scales[:].rearrange("p g c -> p (g c)"),
            in_=w2_grp[:].rearrange("p g c t -> p (g c t)"),
        )

        for step in range(N_BLOCKS + LAG_READ_OUT):
            load_x(step + LOAD_AHEAD)
            regroup_r(step - LAG_READ_OUT)
            quantise_x(step + 1)
            quantise_r(step - LAG_READ_OUT)
            normalise(step - LAG_NORMALISE)
            for i in range(TILES):
                for n in range(HALVES):
                    first_matmul(step, i, n)
                squared_deviations(step - LAG_DEVIATION, i)
                for n in range(HALVES):
                    transpose_and_activate(step - LAG_TRANSPOSE, i * HALVES + n)
                transpose_x(step + X_AHEAD, i)
                if i < TILES - 1:
                    copy_x(nc.scalar.copy, step + X_AHEAD, i)
            second_matmul(step - LAG_READ_OUT)
            standard_deviation(step - LAG_DEVIATION)
            add_bias(step)
            copy_x(nc.vector.tensor_copy, step + X_AHEAD, TILES - 1)
            node_maxima(step - LAG_READ_OUT)

        for cc in range(G_TILES):
            nc.vector.tensor_scalar_add(
                out=node_max[:, cc, :], in0=node_max[:, cc, :], scalar1=b2_col[:, cc : cc + 1]
            )
        maxT_ps = psum.tile([P, P], F32, tag="xT", bufs=1)
        nc.tensor.transpose(maxT_ps[:], node_max[:].rearrange("p c b -> p (c b)"), ident[:])
        result = const.tile([P, 2, P], F32)
        for rep in range(2):
            nc.vector.tensor_copy(out=result[:, rep, :], in_=maxT_ps[:])
        out_view = out.rearrange("b (r c j) -> c b r j", r=2, c=G_TILES)
        n_lines = TOKENS // NODES
        for cc in range(G_TILES):
            nc.sync.dma_start(
                out=out_view[cc], in_=result[cc * n_lines : (cc + 1) * n_lines, :, :]
            )
